import numpy as np
import ml_dtypes


def mxq(x, axis, fmt="e4m3"):
    dtype, down = {"e4m3": (ml_dtypes.float8_e4m3fn, 7), "e5m2": (ml_dtypes.float8_e5m2, 14)}[fmt]
    v = np.moveaxis(np.asarray(x, np.float32).astype(ml_dtypes.bfloat16).astype(np.float64), axis, -1)
    blocks = v.reshape(v.shape[:-1] + (-1, 32))
    amax = np.abs(blocks).max(-1, keepdims=True)
    byte = np.maximum(np.where(amax > 0, np.frexp(amax)[1] - 1 + 127, 0) - down, 1)
    scale = np.exp2(byte - 127.0)
    codes = (blocks / scale).astype(np.float32).astype(dtype).astype(np.float64)
    return np.moveaxis((codes * scale).reshape(v.shape), -1, axis)


WIDE = False


def mx_kscale(k):
    if not WIDE:
        return np.ones(k)
    levels = np.array([10, -10, 5, -5, 0])
    a = np.random.permutation(np.resize(levels, k // 512 * 4)).reshape(k // 512, 4)
    idx = np.arange(k)
    return np.exp2(a[idx // 512, idx % 128 // 32])


BF16 = ml_dtypes.bfloat16


def bf(x):
    return np.asarray(x, np.float32).astype(BF16)


def f64(x):
    return np.asarray(x).astype(np.float64)


E2M1 = np.array([0.0, 0.5, 1.0, 1.5, 2.0, 3.0, 4.0, 6.0, -0.0, -0.5, -1.0, -1.5, -2.0, -3.0, -4.0, -6.0])


def pack_weight(w, fmt):
    k, n = w.shape
    w = f64(bf(w)).reshape(k // 32, 32, n)
    amax = np.abs(w).max(1)
    if fmt == "e4m3":
        byte = np.frexp(amax)[1] - 1 + 127 - 7
    else:
        mant, ex = np.frexp(amax / 6.0)
        byte = np.where(mant > 0.5, ex, ex - 1) + 127
    byte = np.clip(np.where(amax > 0, byte, 1), 1, 254)
    scaled = (w * np.exp2(127.0 - byte)[:, None, :]).reshape(k, n).astype(np.float32)
    by_word = np.ascontiguousarray(scaled.reshape(k // 512, 128, 4, n).transpose(0, 1, 3, 2))
    if fmt == "e4m3":
        words = by_word.astype(ml_dtypes.float8_e4m3fn).view(np.uint8)
    else:
        c = by_word.astype(ml_dtypes.float4_e2m1fn).view(np.uint8) & 0xF
        words = c[..., 0::2] | (c[..., 1::2] << 4)
    return np.ascontiguousarray(words), np.ascontiguousarray(byte.astype(np.uint8).reshape(k // 512, 16, n))


def unpack_weight(words, scales, fmt):
    g, p, n, _ = words.shape
    if fmt == "e4m3":
        vals = np.ascontiguousarray(words).view(ml_dtypes.float8_e4m3fn).astype(np.float64)
    else:
        nib = np.empty((g, p, n, 4), np.uint8)
        nib[..., 0::2] = words & 0xF
        nib[..., 1::2] = words >> 4
        vals = E2M1[nib]
    vals = vals * np.repeat(np.exp2(scales.astype(np.float64) - 127.0), 8, axis=1)[..., None]
    return vals.transpose(0, 1, 3, 2).reshape(g * 512, n)

def pack4(w):
    words, scales = pack_weight(w, "e2m1")
    return words.reshape(words.shape[0], 128, -1), scales


def unpack4(words, scales):
    return unpack_weight(words.reshape(words.shape[0], 128, -1, 2), scales, "e2m1")


B, S, D_IN, D_OUT = 8, 2048, 512, 128


def relative_shift(x):
    b, s, d = x.shape
    padded = np.concatenate([np.zeros((b, 1, d)), x], axis=1).reshape(s + 1, b, d)
    return padded[1:].reshape(b, s, d)


def setup_inputs():
    s = mx_kscale(D_IN)
    pos_embed = bf(np.random.standard_normal((B, S, D_IN)) * s)
    w = np.random.standard_normal((D_OUT, D_IN)) * 1.2 / np.sqrt(D_IN) / s[None, :]
    words, scales = pack4(np.ascontiguousarray(w.T))
    b_r = bf(np.random.standard_normal(D_OUT) * 0.3)
    return {"pos_embed": pos_embed,
            "W_r_words": words,
            "W_r_scales": scales,
            "b_r": b_r}


def reference(pos_embed, W_r_words, W_r_scales, b_r):
    shifted = relative_shift(f64(pos_embed))
    return (mxq(shifted, 2, "e4m3") @ unpack4(W_r_words, W_r_scales)) + f64(b_r)

@@ -1,0 +1,168 @@
+from contextlib import ExitStack
+
+import concourse.mybir as mybir
+from concourse.masks import make_identity
+
+BF16 = mybir.dt.bfloat16
+F32 = mybir.dt.float32
+I32 = mybir.dt.int32
+U32 = mybir.dt.uint32
+U8 = mybir.dt.uint8
+FP8X4 = mybir.dt.float8_e4m3fn_x4
+FP4X4 = mybir.dt.float4_e2m1fn_x4
+
+BATCH, SEQ, D_IN, D_OUT = 8, 2048, 512, 128
+ROWS = BATCH * SEQ
+FLOPS = 2 * ROWS * D_IN * D_OUT
+
+P = 128
+PACK = 4
+WORDS = D_IN // 2
+DROPPED = BATCH
+UNUSED = DROPPED - 1
+ZERO_ROWS = BATCH - 1
+
+SLOTS = 8
+CHUNK_ROWS = P * SLOTS
+CHUNKS = ROWS // CHUNK_ROWS
+CHUNKS_PER_BATCH = SEQ // CHUNK_ROWS
+ZERO_CHUNK = CHUNKS_PER_BATCH - 1
+FIRST_ZERO_SLOT = SLOTS - ZERO_ROWS
+assert ZERO_ROWS == UNUSED and ZERO_ROWS < SLOTS
+SLOTS_PER_FLIP_BANK = 2
+SLOTS_PER_SUM_BANK = 4
+CHUNKS_AHEAD = 8
+
+
+def first_rows(j):
+    batch = j // CHUNKS_PER_BATCH
+    first_input = j * CHUNK_ROWS + (UNUSED if batch == 0 else 0)
+    return first_input, first_input + batch - UNUSED
+
+
+def tile_relativemultiheadattention_pa_t_kernel(tc, pos_embed, W_r_words, W_r_scales, b_r, out):
+    nc = tc.nc
+    x_dram = pos_embed.flatten_outer_dims()
+    out_dram = out.flatten_outer_dims()
+
+    with ExitStack() as ctx:
+        const = ctx.enter_context(tc.tile_pool(name="const", bufs=1))
+        x_pool = ctx.enter_context(tc.tile_pool(name="x", bufs=CHUNKS_AHEAD))
+        grouped_pool = ctx.enter_context(tc.tile_pool(name="grouped", bufs=3))
+        codes_pool = ctx.enter_context(tc.tile_pool(name="codes", bufs=3))
+        result_pool = ctx.enter_context(tc.tile_pool(name="result", bufs=4))
+        flip_psum = ctx.enter_context(tc.psum_pool(name="flip", bufs=6))
+        sum_psum = ctx.enter_context(tc.psum_pool(name="sum", bufs=2))
+        ctx.enter_context(tc.manual_schedule())
+
+        x_tiles = {}
+        grouped_tiles = {}
+        code_tiles = {}
+
+        def load_chunk(j, pieces):
+            first_input = first_rows(j)[0]
+            rows = x_dram[first_input : first_input + CHUNK_ROWS, :].rearrange("(p t) k -> p t k", t=SLOTS)
+            x_rows = x_pool.tile([P, SLOTS, D_IN], BF16, name="x_rows")
+            width = SLOTS // pieces
+            for t in range(0, SLOTS, width):
+                nc.sync.dma_start(
+                    out=x_rows[:, t : t + width, :].rearrange("p t k -> p (t k)"),
+                    in_=rows[:, t : t + width, :].rearrange("p t k -> p (t k)"),
+                )
+            x_tiles[j] = x_rows
+
+        def transpose_chunk(j):
+            x_words = x_tiles.pop(j)[:].bitcast(F32)
+            grouped = grouped_pool.tile([P, SLOTS * D_IN], BF16, name="grouped", align_bytes=64)
+            grouped_words = grouped[:].bitcast(F32).rearrange("p (t r u) -> p t r u", t=SLOTS, u=2)
+            for first_slot in range(0, SLOTS, SLOTS_PER_FLIP_BANK):
+                flipped = flip_psum.tile([P, SLOTS_PER_FLIP_BANK, 2, P], F32, name="flipped")
+                for s in range(SLOTS_PER_FLIP_BANK):
+                    for u in range(2):
+                        nc.tensor.transpose(flipped[:, s, u, :], x_words[:, first_slot + s, u:WORDS:2], identity[:])
+                nc.scalar.copy(
+                    out=grouped_words[:, first_slot : first_slot + SLOTS_PER_FLIP_BANK, :, :],
+                    in_=flipped[:].rearrange("p s u r -> p s r u"),
+                )
+            grouped_tiles[j] = grouped
+
+        def quantise_chunk(j):
+            grouped = grouped_tiles.pop(j)
+            if j == ZERO_CHUNK:
+                by_row = grouped[:].rearrange("p (t r v) -> p t r v", t=SLOTS, v=PACK)
+                nc.vector.memset(by_row[:, FIRST_ZERO_SLOT:, P - 1, :], 0.0)
+            codes = codes_pool.tile([P, SLOTS * P], U32, name="codes", align_bytes=64)
+            scales = codes_pool.tile([P, SLOTS * P], U8, name="scales", align_bytes=64)
+            half = SLOTS * P // 2
+            for start in (0, half):
+                nc.vector.quantize_mx(
+                    out=codes[:, start : start + half].bitcast(FP8X4),
+                    scales=scales[:, start : start + half],
+                    in_=grouped[:, PACK * start : PACK * (start + half)],
+                )
+            code_tiles[j] = (codes, scales)
+
+        def multiply_chunk(j):
+            codes, scales = code_tiles.pop(j)
+            result = result_pool.tile([P, SLOTS, D_OUT], F32, name="result")
+            for first_slot in range(0, SLOTS, SLOTS_PER_SUM_BANK):
+                sums = sum_psum.tile([P, SLOTS_PER_SUM_BANK, D_OUT], F32, name="sums")
+                for s in range(SLOTS_PER_SUM_BANK):
+                    cols = slice((first_slot + s) * P, (first_slot + s + 1) * P)
+                    nc.tensor.matmul_mx(
+                        out=sums[:, s, :],
+                        lhsT=codes[:, cols].bitcast(FP8X4),
+                        lhsT_scale=scales[:, cols],
+                        rhs=w_words[:].bitcast(FP4X4),
+                        rhs_scale=w_scales[:],
+                        start=True,
+                        stop=True,
+                    )
+                nc.vector.tensor_tensor(
+                    out=result[:, first_slot : first_slot + SLOTS_PER_SUM_BANK, :],
+                    in0=sums[:],
+                    in1=bias[:].unsqueeze(1).to_broadcast([P, SLOTS_PER_SUM_BANK, D_OUT]),
+                    op=mybir.AluOpType.add,
+                )
+            first_output = first_rows(j)[1]
+            nc.sync.dma_start(
+                out=out_dram[first_output : first_output + CHUNK_ROWS, :].rearrange("(p t) n -> p (t n)", t=SLOTS),
+                in_=result[:].rearrange("p t n -> p (t n)"),
+            )
+            if j == ZERO_CHUNK:
+                second = 2 * (SEQ + 1) - DROPPED
+                nc.sync.dma_start(
+                    out=out_dram[second : second + (ZERO_ROWS - 2) * (SEQ + 1) + 1 : SEQ + 1, :].unsqueeze(0),
+                    in_=result[P - 1 : P, FIRST_ZERO_SLOT + 1 :, :],
+                )
+
+        identity = const.tile([P, P], F32, name="identity")
+        make_identity(nc, identity[:])
+        w_words = const.tile([P, 2 * D_OUT], U8, name="w_words", align_bytes=64)
+        w_scales = const.tile([P, D_OUT], U8, name="w_scales", align_bytes=64)
+        bias_bf16 = const.tile([P, D_OUT], BF16, name="bias_bf16")
+        bias = const.tile([P, D_OUT], F32, name="bias")
+        nc.vector.memset(w_scales[:].bitcast(I32), 0)
+
+        load_chunk(0, SLOTS // SLOTS_PER_FLIP_BANK)
+        load_chunk(1, 1)
+        nc.sync.dma_start(out=w_words[:].bitcast(I32), in_=W_r_words[0].bitcast(I32))
+        for quadrant in range(4):
+            nc.sync.dma_start(
+                out=w_scales[32 * quadrant : 32 * quadrant + 4, :].bitcast(I32),
+                in_=W_r_scales[0, 4 * quadrant : 4 * quadrant + 4, :].bitcast(I32),
+            )
+        nc.sync.dma_start(out=bias_bf16[:], in_=b_r.partition_broadcast(P))
+        for j in range(2, CHUNKS_AHEAD):
+            load_chunk(j, 1)
+        nc.vector.tensor_copy(out=bias[:], in_=bias_bf16[:])
+
+        for step in range(CHUNKS + 2):
+            if step < CHUNKS:
+                transpose_chunk(step)
+                if step + CHUNKS_AHEAD < CHUNKS:
+                    load_chunk(step + CHUNKS_AHEAD, 1)
+            if 1 <= step <= CHUNKS:
+                quantise_chunk(step - 1)
+            if step >= 2:
+                multiply_chunk(step - 2)

@@ -31,7 +31,7 @@ FIRST_ZERO_SLOT = SLOTS - ZERO_ROWS
 assert ZERO_ROWS == UNUSED and ZERO_ROWS < SLOTS
 SLOTS_PER_FLIP_BANK = 2
 SLOTS_PER_SUM_BANK = 4
-CHUNKS_AHEAD = 8
+CHUNKS_AHEAD = CHUNKS
 
 
 def first_rows(j):
@@ -48,9 +48,9 @@ def tile_relativemultiheadattention_pa_t_kernel(tc, pos_embed, W_r_words, W_r_sc
     with ExitStack() as ctx:
         const = ctx.enter_context(tc.tile_pool(name="const", bufs=1))
         x_pool = ctx.enter_context(tc.tile_pool(name="x", bufs=CHUNKS_AHEAD))
-        grouped_pool = ctx.enter_context(tc.tile_pool(name="grouped", bufs=3))
+        grouped_pool = ctx.enter_context(tc.tile_pool(name="grouped", bufs=2))
         codes_pool = ctx.enter_context(tc.tile_pool(name="codes", bufs=3))
-        result_pool = ctx.enter_context(tc.tile_pool(name="result", bufs=4))
+        result_pool = ctx.enter_context(tc.tile_pool(name="result", bufs=CHUNKS))
         flip_psum = ctx.enter_context(tc.psum_pool(name="flip", bufs=6))
         sum_psum = ctx.enter_context(tc.psum_pool(name="sum", bufs=2))
         ctx.enter_context(tc.manual_schedule())

@@ -125,13 +125,14 @@ def tile_relativemultiheadattention_pa_t_kernel(tc, pos_embed, W_r_words, W_r_sc
                     op=mybir.AluOpType.add,
                 )
             first_output = first_rows(j)[1]
-            nc.sync.dma_start(
+            queue = nc.gpsimd if j == ZERO_CHUNK else nc.sync
+            queue.dma_start(
                 out=out_dram[first_output : first_output + CHUNK_ROWS, :].rearrange("(p t) n -> p (t n)", t=SLOTS),
                 in_=result[:].rearrange("p t n -> p (t n)"),
             )
             if j == ZERO_CHUNK:
                 second = 2 * (SEQ + 1) - DROPPED
-                nc.sync.dma_start(
+                queue.dma_start(
                     out=out_dram[second : second + (ZERO_ROWS - 2) * (SEQ + 1) + 1 : SEQ + 1, :].unsqueeze(0),
                     in_=result[P - 1 : P, FIRST_ZERO_SLOT + 1 :, :],
                 )

@@ -22,22 +22,20 @@ DROPPED = BATCH
 UNUSED = DROPPED - 1
 ZERO_ROWS = BATCH - 1
 
-SLOTS = 8
-CHUNK_ROWS = P * SLOTS
-CHUNKS = ROWS // CHUNK_ROWS
-CHUNKS_PER_BATCH = SEQ // CHUNK_ROWS
-ZERO_CHUNK = CHUNKS_PER_BATCH - 1
+SLOTS = SEQ // P
 FIRST_ZERO_SLOT = SLOTS - ZERO_ROWS
-assert ZERO_ROWS == UNUSED and ZERO_ROWS < SLOTS
+ROUND_SLOTS = 8
+ROUNDS_PER_CHUNK = SLOTS // ROUND_SLOTS
+ROUNDS = BATCH * ROUNDS_PER_CHUNK
+ZERO_ROUND = ROUNDS_PER_CHUNK - 1
+assert ZERO_ROWS == UNUSED and ZERO_ROWS < ROUND_SLOTS
 SLOTS_PER_FLIP_BANK = 2
 SLOTS_PER_SUM_BANK = 4
-CHUNKS_AHEAD = CHUNKS
 
 
-def first_rows(j):
-    batch = j // CHUNKS_PER_BATCH
-    first_input = j * CHUNK_ROWS + (UNUSED if batch == 0 else 0)
-    return first_input, first_input + batch - UNUSED
+def first_rows(chunk):
+    first_input = chunk * SEQ + (UNUSED if chunk == 0 else 0)
+    return first_input, first_input + chunk - UNUSED
 
 
 def tile_relativemultiheadattention_pa_t_kernel(tc, pos_embed, W_r_words, W_r_scales, b_r, out):
@@ -47,10 +45,10 @@ def tile_relativemultiheadattention_pa_t_kernel(tc, pos_embed, W_r_words, W_r_sc
 
     with ExitStack() as ctx:
         const = ctx.enter_context(tc.tile_pool(name="const", bufs=1))
-        x_pool = ctx.enter_context(tc.tile_pool(name="x", bufs=CHUNKS_AHEAD))
+        x_pool = ctx.enter_context(tc.tile_pool(name="x", bufs=BATCH))
+        result_pool = ctx.enter_context(tc.tile_pool(name="result", bufs=BATCH))
         grouped_pool = ctx.enter_context(tc.tile_pool(name="grouped", bufs=2))
         codes_pool = ctx.enter_context(tc.tile_pool(name="codes", bufs=3))
-        result_pool = ctx.enter_context(tc.tile_pool(name="result", bufs=CHUNKS))
         flip_psum = ctx.enter_context(tc.psum_pool(name="flip", bufs=6))
         sum_psum = ctx.enter_context(tc.psum_pool(name="sum", bufs=2))
         ctx.enter_context(tc.manual_schedule())
@@ -58,57 +56,74 @@ def tile_relativemultiheadattention_pa_t_kernel(tc, pos_embed, W_r_words, W_r_sc
         x_tiles = {}
         grouped_tiles = {}
         code_tiles = {}
+        result_tiles = {}
 
-        def load_chunk(j, pieces):
-            first_input = first_rows(j)[0]
-            rows = x_dram[first_input : first_input + CHUNK_ROWS, :].rearrange("(p t) k -> p t k", t=SLOTS)
+        def load_chunk(chunk, first_piece):
+            first_input = first_rows(chunk)[0]
+            x_view = x_dram[first_input : first_input + SEQ, :].rearrange("(p t) k -> p t k", t=SLOTS)
             x_rows = x_pool.tile([P, SLOTS, D_IN], BF16, name="x_rows")
-            width = SLOTS // pieces
-            for t in range(0, SLOTS, width):
+            t, width = 0, first_piece
+            while t < SLOTS:
                 nc.sync.dma_start(
                     out=x_rows[:, t : t + width, :].rearrange("p t k -> p (t k)"),
-                    in_=rows[:, t : t + width, :].rearrange("p t k -> p (t k)"),
+                    in_=x_view[:, t : t + width, :].rearrange("p t k -> p (t k)"),
                 )
-            x_tiles[j] = x_rows
+                t += width
+                width = t
+            x_tiles[chunk] = x_rows
 
-        def transpose_chunk(j):
-            x_words = x_tiles.pop(j)[:].bitcast(F32)
-            grouped = grouped_pool.tile([P, SLOTS * D_IN], BF16, name="grouped", align_bytes=64)
-            grouped_words = grouped[:].bitcast(F32).rearrange("p (t r u) -> p t r u", t=SLOTS, u=2)
-            for first_slot in range(0, SLOTS, SLOTS_PER_FLIP_BANK):
+        def transpose_round(i):
+            chunk, part = divmod(i, ROUNDS_PER_CHUNK)
+            x_words = x_tiles[chunk][:].bitcast(F32)
+            grouped = grouped_pool.tile([P, ROUND_SLOTS * D_IN], BF16, name="grouped", align_bytes=64)
+            grouped_words = grouped[:].bitcast(F32).rearrange("p (t r u) -> p t r u", t=ROUND_SLOTS, u=2)
+            for t in range(0, ROUND_SLOTS, SLOTS_PER_FLIP_BANK):
                 flipped = flip_psum.tile([P, SLOTS_PER_FLIP_BANK, 2, P], F32, name="flipped")
                 for s in range(SLOTS_PER_FLIP_BANK):
                     for u in range(2):
-                        nc.tensor.transpose(flipped[:, s, u, :], x_words[:, first_slot + s, u:WORDS:2], identity[:])
+                        nc.tensor.transpose(
+                            flipped[:, s, u, :], x_words[:, part * ROUND_SLOTS + t + s, u:WORDS:2], identity[:]
+                        )
                 nc.scalar.copy(
-                    out=grouped_words[:, first_slot : first_slot + SLOTS_PER_FLIP_BANK, :, :],
+                    out=grouped_words[:, t : t + SLOTS_PER_FLIP_BANK, :, :],
                     in_=flipped[:].rearrange("p s u r -> p s r u"),
                 )
-            grouped_tiles[j] = grouped
+            grouped_tiles[i] = grouped
 
-        def quantise_chunk(j):
-            grouped = grouped_tiles.pop(j)
-            if j == ZERO_CHUNK:
-                by_row = grouped[:].rearrange("p (t r v) -> p t r v", t=SLOTS, v=PACK)
-                nc.vector.memset(by_row[:, FIRST_ZERO_SLOT:, P - 1, :], 0.0)
-            codes = codes_pool.tile([P, SLOTS * P], U32, name="codes", align_bytes=64)
-            scales = codes_pool.tile([P, SLOTS * P], U8, name="scales", align_bytes=64)
-            half = SLOTS * P // 2
-            for start in (0, half):
+        def quantise_round(i):
+            grouped = grouped_tiles.pop(i)
+            if i == ZERO_ROUND:
+                by_row = grouped[:].rearrange("p (t r v) -> p t r v", t=ROUND_SLOTS, v=PACK)
+                nc.vector.memset(by_row[:, ROUND_SLOTS - ZERO_ROWS :, P - 1, :], 0.0)
+            codes = codes_pool.tile([P, ROUND_SLOTS * P], U32, name="codes", align_bytes=64)
+            scales = codes_pool.tile([P, ROUND_SLOTS * P], U8, name="scales", align_bytes=64)
+            width = SLOTS_PER_SUM_BANK * P
+            for c in range(0, ROUND_SLOTS * P, width):
                 nc.vector.quantize_mx(
-                    out=codes[:, start : start + half].bitcast(FP8X4),
-                    scales=scales[:, start : start + half],
-                    in_=grouped[:, PACK * start : PACK * (start + half)],
+                    out=codes[:, c : c + width].bitcast(FP8X4),
+                    scales=scales[:, c : c + width],
+                    in_=grouped[:, PACK * c : PACK * (c + width)],
                 )
-            code_tiles[j] = (codes, scales)
+            code_tiles[i] = (codes, scales)
 
-        def multiply_chunk(j):
-            codes, scales = code_tiles.pop(j)
-            result = result_pool.tile([P, SLOTS, D_OUT], F32, name="result")
-            for first_slot in range(0, SLOTS, SLOTS_PER_SUM_BANK):
+        def store(chunk, first_slot, slots, queue):
+            first_output = first_rows(chunk)[1]
+            out_view = out_dram[first_output : first_output + SEQ, :].rearrange("(p t) n -> p t n", t=SLOTS)
+            queue.dma_start(
+                out=out_view[:, first_slot : first_slot + slots, :],
+                in_=result_tiles[chunk][:, first_slot : first_slot + slots, :],
+            )
+
+        def multiply_round(i):
+            chunk, part = divmod(i, ROUNDS_PER_CHUNK)
+            codes, scales = code_tiles.pop(i)
+            if part == 0:
+                result = result_pool.tile([P, SLOTS, D_OUT], F32, name="result")
+                result_tiles[chunk] = result
+            for t in range(0, ROUND_SLOTS, SLOTS_PER_SUM_BANK):
                 sums = sum_psum.tile([P, SLOTS_PER_SUM_BANK, D_OUT], F32, name="sums")
                 for s in range(SLOTS_PER_SUM_BANK):
-                    cols = slice((first_slot + s) * P, (first_slot + s + 1) * P)
+                    cols = slice((t + s) * P, (t + s + 1) * P)
                     nc.tensor.matmul_mx(
                         out=sums[:, s, :],
                         lhsT=codes[:, cols].bitcast(FP8X4),
@@ -118,52 +133,64 @@ def tile_relativemultiheadattention_pa_t_kernel(tc, pos_embed, W_r_words, W_r_sc
                         start=True,
                         stop=True,
                     )
+                first_slot = part * ROUND_SLOTS + t
                 nc.vector.tensor_tensor(
-                    out=result[:, first_slot : first_slot + SLOTS_PER_SUM_BANK, :],
+                    out=result_tiles[chunk][:, first_slot : first_slot + SLOTS_PER_SUM_BANK, :],
                     in0=sums[:],
-                    in1=bias[:].unsqueeze(1).to_broadcast([P, SLOTS_PER_SUM_BANK, D_OUT]),
+                    in1=bias[:],
                     op=mybir.AluOpType.add,
                 )
-            first_output = first_rows(j)[1]
-            queue = nc.gpsimd if j == ZERO_CHUNK else nc.sync
-            queue.dma_start(
-                out=out_dram[first_output : first_output + CHUNK_ROWS, :].rearrange("(p t) n -> p (t n)", t=SLOTS),
-                in_=result[:].rearrange("p t n -> p (t n)"),
-            )
-            if j == ZERO_CHUNK:
+            if chunk == BATCH - 1:
+                store(chunk, part * ROUND_SLOTS, ROUND_SLOTS, nc.sync)
+            elif i == ZERO_ROUND:
+                store(chunk, 0, SLOTS, nc.gpsimd)
                 second = 2 * (SEQ + 1) - DROPPED
-                queue.dma_start(
+                nc.gpsimd.dma_start(
                     out=out_dram[second : second + (ZERO_ROWS - 2) * (SEQ + 1) + 1 : SEQ + 1, :].unsqueeze(0),
-                    in_=result[P - 1 : P, FIRST_ZERO_SLOT + 1 :, :],
+                    in_=result_tiles[chunk][P - 1 : P, FIRST_ZERO_SLOT + 1 :, :],
                 )
+            elif part == ROUNDS_PER_CHUNK - 1:
+                store(chunk, 0, SLOTS, nc.sync)
+
+        def spread_bias():
+            spread = sum_psum.tile([P, SLOTS_PER_SUM_BANK, D_OUT], F32, name="sums")
+            nc.tensor.matmul(
+                out=spread[:].rearrange("p s n -> p (s n)"), lhsT=ones[:], rhs=bias_rows[:], start=True, stop=True
+            )
+            nc.vector.tensor_copy(out=bias[:], in_=spread[:])
 
         identity = const.tile([P, P], F32, name="identity")
         make_identity(nc, identity[:])
         w_words = const.tile([P, 2 * D_OUT], U8, name="w_words", align_bytes=64)
         w_scales = const.tile([P, D_OUT], U8, name="w_scales", align_bytes=64)
-        bias_bf16 = const.tile([P, D_OUT], BF16, name="bias_bf16")
-        bias = const.tile([P, D_OUT], F32, name="bias")
+        ones = const.tile([P, P], BF16, name="ones")
+        bias_rows = const.tile([P, SLOTS_PER_SUM_BANK * D_OUT], BF16, name="bias_rows")
+        bias = const.tile([P, SLOTS_PER_SUM_BANK, D_OUT], F32, name="bias")
         nc.vector.memset(w_scales[:].bitcast(I32), 0)
+        nc.vector.memset(ones[:], 1.0)
+        nc.vector.memset(bias_rows[:], 0.0)
 
-        load_chunk(0, SLOTS // SLOTS_PER_FLIP_BANK)
-        load_chunk(1, 1)
+        load_chunk(0, SLOTS_PER_FLIP_BANK)
+        load_chunk(1, SLOTS)
         nc.sync.dma_start(out=w_words[:].bitcast(I32), in_=W_r_words[0].bitcast(I32))
         for quadrant in range(4):
             nc.sync.dma_start(
                 out=w_scales[32 * quadrant : 32 * quadrant + 4, :].bitcast(I32),
                 in_=W_r_scales[0, 4 * quadrant : 4 * quadrant + 4, :].bitcast(I32),
             )
-        nc.sync.dma_start(out=bias_bf16[:], in_=b_r.partition_broadcast(P))
-        for j in range(2, CHUNKS_AHEAD):
-            load_chunk(j, 1)
-        nc.vector.tensor_copy(out=bias[:], in_=bias_bf16[:])
+        nc.sync.dma_start(
+            out=bias_rows[0:1, :].rearrange("o (s n) -> o s n", s=SLOTS_PER_SUM_BANK),
+            in_=b_r.unsqueeze(0).unsqueeze(0).to_broadcast([1, SLOTS_PER_SUM_BANK, D_OUT]),
+        )
+        for chunk in range(2, BATCH):
+            load_chunk(chunk, SLOTS)
 
-        for step in range(CHUNKS + 2):
-            if step < CHUNKS:
-                transpose_chunk(step)
-                if step + CHUNKS_AHEAD < CHUNKS:
-                    load_chunk(step + CHUNKS_AHEAD, 1)
-            if 1 <= step <= CHUNKS:
-                quantise_chunk(step - 1)
+        for step in range(ROUNDS + 2):
+            if step < ROUNDS:
+                transpose_round(step)
+            if 1 <= step <= ROUNDS:
+                quantise_round(step - 1)
+            if step == 2:
+                spread_bias()
             if step >= 2:
-                multiply_chunk(step - 2)
+                multiply_round(step - 2)

@@ -58,19 +58,16 @@ def tile_relativemultiheadattention_pa_t_kernel(tc, pos_embed, W_r_words, W_r_sc
         code_tiles = {}
         result_tiles = {}
 
-        def load_chunk(chunk, first_piece):
+        def load_slots(chunk, t, width):
+            if t == 0:
+                x_rows = x_pool.tile([P, SLOTS, D_IN], BF16, name="x_rows")
+                x_tiles[chunk] = x_rows
             first_input = first_rows(chunk)[0]
             x_view = x_dram[first_input : first_input + SEQ, :].rearrange("(p t) k -> p t k", t=SLOTS)
-            x_rows = x_pool.tile([P, SLOTS, D_IN], BF16, name="x_rows")
-            t, width = 0, first_piece
-            while t < SLOTS:
-                nc.sync.dma_start(
-                    out=x_rows[:, t : t + width, :].rearrange("p t k -> p (t k)"),
-                    in_=x_view[:, t : t + width, :].rearrange("p t k -> p (t k)"),
-                )
-                t += width
-                width = t
-            x_tiles[chunk] = x_rows
+            nc.sync.dma_start(
+                out=x_tiles[chunk][:, t : t + width, :].rearrange("p t k -> p (t k)"),
+                in_=x_view[:, t : t + width, :].rearrange("p t k -> p (t k)"),
+            )
 
         def transpose_round(i):
             chunk, part = divmod(i, ROUNDS_PER_CHUNK)
@@ -82,7 +79,7 @@ def tile_relativemultiheadattention_pa_t_kernel(tc, pos_embed, W_r_words, W_r_sc
                 for s in range(SLOTS_PER_FLIP_BANK):
                     for u in range(2):
                         nc.tensor.transpose(
-                            flipped[:, s, u, :], x_words[:, part * ROUND_SLOTS + t + s, u:WORDS:2], identity[:]
+                            flipped[:, s, u, :], x_words[:, part * ROUND_SLOTS + t + s, u * P : (u + 1) * P], identity[:]
                         )
                 nc.scalar.copy(
                     out=grouped_words[:, t : t + SLOTS_PER_FLIP_BANK, :, :],
@@ -124,15 +121,16 @@ def tile_relativemultiheadattention_pa_t_kernel(tc, pos_embed, W_r_words, W_r_sc
                 sums = sum_psum.tile([P, SLOTS_PER_SUM_BANK, D_OUT], F32, name="sums")
                 for s in range(SLOTS_PER_SUM_BANK):
                     cols = slice((t + s) * P, (t + s + 1) * P)
-                    nc.tensor.matmul_mx(
-                        out=sums[:, s, :],
-                        lhsT=codes[:, cols].bitcast(FP8X4),
-                        lhsT_scale=scales[:, cols],
-                        rhs=w_words[:].bitcast(FP4X4),
-                        rhs_scale=w_scales[:],
-                        start=True,
-                        stop=True,
-                    )
+                    for h in range(2):
+                        nc.tensor.matmul_mx(
+                            out=sums[:, s, :],
+                            lhsT=codes[:, cols].bitcast(FP8X4),
+                            lhsT_scale=scales[:, cols],
+                            rhs=w_half[:, 2 * D_OUT * h : 2 * D_OUT * (h + 1)].bitcast(FP4X4),
+                            rhs_scale=w_scales[:, D_OUT * h : D_OUT * (h + 1)],
+                            start=(h == 0),
+                            stop=(h == 1),
+                        )
                 first_slot = part * ROUND_SLOTS + t
                 nc.vector.tensor_tensor(
                     out=result_tiles[chunk][:, first_slot : first_slot + SLOTS_PER_SUM_BANK, :],
@@ -161,29 +159,48 @@ def tile_relativemultiheadattention_pa_t_kernel(tc, pos_embed, W_r_words, W_r_sc
 
         identity = const.tile([P, P], F32, name="identity")
         make_identity(nc, identity[:])
-        w_words = const.tile([P, 2 * D_OUT], U8, name="w_words", align_bytes=64)
-        w_scales = const.tile([P, D_OUT], U8, name="w_scales", align_bytes=64)
+        w_raw = const.tile([P, D_OUT * 2], U8, name="w_raw", align_bytes=64)
+        w_planes = const.tile([P, 2 * D_OUT], U8, name="w_planes", align_bytes=64)
+        w_unzipped = const.tile([P, 2 * D_OUT], U8, name="w_unzipped", align_bytes=64)
+        w_half = const.tile([P, 2 * D_OUT * 2], U8, name="w_half", align_bytes=64)
+        w_scales = const.tile([P, 2 * D_OUT], U8, name="w_scales", align_bytes=64)
         ones = const.tile([P, P], BF16, name="ones")
         bias_rows = const.tile([P, SLOTS_PER_SUM_BANK * D_OUT], BF16, name="bias_rows")
         bias = const.tile([P, SLOTS_PER_SUM_BANK, D_OUT], F32, name="bias")
         nc.vector.memset(w_scales[:].bitcast(I32), 0)
+        nc.vector.memset(w_half[:].bitcast(I32), 0)
         nc.vector.memset(ones[:], 1.0)
         nc.vector.memset(bias_rows[:], 0.0)
 
-        load_chunk(0, SLOTS_PER_FLIP_BANK)
-        load_chunk(1, SLOTS)
-        nc.sync.dma_start(out=w_words[:].bitcast(I32), in_=W_r_words[0].bitcast(I32))
-        for quadrant in range(4):
+        load_slots(0, 0, 2)
+        nc.sync.dma_start(out=w_raw[:].bitcast(I32), in_=W_r_words[0].bitcast(I32))
+        scale_rows = W_r_scales[0].rearrange("(h g j) n -> j g h n", h=2, g=4, j=2)
+        for i in range(4):
             nc.sync.dma_start(
-                out=w_scales[32 * quadrant : 32 * quadrant + 4, :].bitcast(I32),
-                in_=W_r_scales[0, 4 * quadrant : 4 * quadrant + 4, :].bitcast(I32),
+                out=w_scales[i:P:32, :].bitcast(I32).rearrange("q (h m) -> q h m", h=2),
+                in_=scale_rows[i // 2].bitcast(I32),
             )
+        load_slots(0, 2, 2)
+        load_slots(0, 4, 4)
+        for c in range(2):
+            nc.vector.tensor_copy(
+                out=w_planes[:, D_OUT * c : D_OUT * (c + 1)], in_=w_raw[:].rearrange("p (n c) -> p n c", c=2)[:, :, c]
+            )
+        for h in range(2):
+            for c in range(2):
+                nc.sync.dma_start(
+                    out=w_unzipped[c:P:2, D_OUT * h : D_OUT * (h + 1)].bitcast(I32),
+                    in_=w_planes[64 * h : 64 * (h + 1), D_OUT * c : D_OUT * (c + 1)].bitcast(I32),
+                )
+        load_slots(0, 8, 8)
         nc.sync.dma_start(
             out=bias_rows[0:1, :].rearrange("o (s n) -> o s n", s=SLOTS_PER_SUM_BANK),
             in_=b_r.unsqueeze(0).unsqueeze(0).to_broadcast([1, SLOTS_PER_SUM_BANK, D_OUT]),
         )
+        load_slots(1, 0, 8)
+        load_slots(1, 8, 8)
         for chunk in range(2, BATCH):
-            load_chunk(chunk, SLOTS)
+            load_slots(chunk, 0, SLOTS)
 
         for step in range(ROUNDS + 2):
             if step < ROUNDS:
@@ -191,6 +208,11 @@ def tile_relativemultiheadattention_pa_t_kernel(tc, pos_embed, W_r_words, W_r_sc
             if 1 <= step <= ROUNDS:
                 quantise_round(step - 1)
             if step == 2:
+                for h in range(2):
+                    nc.vector.tensor_copy(
+                        out=w_half[:, 2 * D_OUT * h : 2 * D_OUT * (h + 1)].rearrange("p (n c) -> p n c", c=2)[:, :, h],
+                        in_=w_unzipped[:, D_OUT * h : D_OUT * (h + 1)],
+                    )
                 spread_bias()
             if step >= 2:
                 multiply_round(step - 2)

@@ -141,14 +141,16 @@ def tile_relativemultiheadattention_pa_t_kernel(tc, pos_embed, W_r_words, W_r_sc
             if chunk == BATCH - 1:
                 store(chunk, part * ROUND_SLOTS, ROUND_SLOTS, nc.sync)
             elif i == ZERO_ROUND:
-                store(chunk, 0, SLOTS, nc.gpsimd)
+                store(chunk, 0, SLOTS, nc.sync)
                 second = 2 * (SEQ + 1) - DROPPED
-                nc.gpsimd.dma_start(
+                nc.sync.dma_start(
                     out=out_dram[second : second + (ZERO_ROWS - 2) * (SEQ + 1) + 1 : SEQ + 1, :].unsqueeze(0),
                     in_=result_tiles[chunk][P - 1 : P, FIRST_ZERO_SLOT + 1 :, :],
                 )
-            elif part == ROUNDS_PER_CHUNK - 1:
+            elif part == ROUNDS_PER_CHUNK - 1 and chunk != 1:
                 store(chunk, 0, SLOTS, nc.sync)
+                if chunk == 3:
+                    store(1, 0, SLOTS, nc.sync)
 
         def spread_bias():
             spread = sum_psum.tile([P, SLOTS_PER_SUM_BANK, D_OUT], F32, name="sums")
@@ -172,16 +174,16 @@ def tile_relativemultiheadattention_pa_t_kernel(tc, pos_embed, W_r_words, W_r_sc
         nc.vector.memset(ones[:], 1.0)
         nc.vector.memset(bias_rows[:], 0.0)
 
-        load_slots(0, 0, 2)
         nc.sync.dma_start(out=w_raw[:].bitcast(I32), in_=W_r_words[0].bitcast(I32))
+        load_slots(0, 0, 2)
         scale_rows = W_r_scales[0].rearrange("(h g j) n -> j g h n", h=2, g=4, j=2)
         for i in range(4):
             nc.sync.dma_start(
                 out=w_scales[i:P:32, :].bitcast(I32).rearrange("q (h m) -> q h m", h=2),
                 in_=scale_rows[i // 2].bitcast(I32),
             )
-        load_slots(0, 2, 2)
-        load_slots(0, 4, 4)
+        load_slots(0, 2, 6)
+        load_slots(0, 8, 8)
         for c in range(2):
             nc.vector.tensor_copy(
                 out=w_planes[:, D_OUT * c : D_OUT * (c + 1)], in_=w_raw[:].rearrange("p (n c) -> p n c", c=2)[:, :, c]
@@ -192,14 +194,14 @@ def tile_relativemultiheadattention_pa_t_kernel(tc, pos_embed, W_r_words, W_r_sc
                     out=w_unzipped[c:P:2, D_OUT * h : D_OUT * (h + 1)].bitcast(I32),
                     in_=w_planes[64 * h : 64 * (h + 1), D_OUT * c : D_OUT * (c + 1)].bitcast(I32),
                 )
-        load_slots(0, 8, 8)
-        nc.sync.dma_start(
+        nc.gpsimd.dma_start(
             out=bias_rows[0:1, :].rearrange("o (s n) -> o s n", s=SLOTS_PER_SUM_BANK),
             in_=b_r.unsqueeze(0).unsqueeze(0).to_broadcast([1, SLOTS_PER_SUM_BANK, D_OUT]),
         )
-        load_slots(1, 0, 8)
-        load_slots(1, 8, 8)
-        for chunk in range(2, BATCH):
+        for chunk in (1, 2, 3):
+            load_slots(chunk, 0, 8)
+            load_slots(chunk, 8, 8)
+        for chunk in range(4, BATCH):
             load_slots(chunk, 0, SLOTS)
 
         for step in range(ROUNDS + 2):

from contextlib import ExitStack

import concourse.mybir as mybir
from concourse.masks import make_identity

BF16 = mybir.dt.bfloat16
F32 = mybir.dt.float32
I32 = mybir.dt.int32
U32 = mybir.dt.uint32
U8 = mybir.dt.uint8
FP8X4 = mybir.dt.float8_e4m3fn_x4
FP4X4 = mybir.dt.float4_e2m1fn_x4

BATCH, SEQ, D_IN, D_OUT = 8, 2048, 512, 128
ROWS = BATCH * SEQ
FLOPS = 2 * ROWS * D_IN * D_OUT

P = 128
PACK = 4
WORDS = D_IN // 2
DROPPED = BATCH
UNUSED = DROPPED - 1
ZERO_ROWS = BATCH - 1

SLOTS = SEQ // P
FIRST_ZERO_SLOT = SLOTS - ZERO_ROWS
ROUND_SLOTS = 8
ROUNDS_PER_CHUNK = SLOTS // ROUND_SLOTS
ROUNDS = BATCH * ROUNDS_PER_CHUNK
ZERO_ROUND = ROUNDS_PER_CHUNK - 1
assert ZERO_ROWS == UNUSED and ZERO_ROWS < ROUND_SLOTS
SLOTS_PER_FLIP_BANK = 2
SLOTS_PER_SUM_BANK = 4


def first_rows(chunk):
    first_input = chunk * SEQ + (UNUSED if chunk == 0 else 0)
    return first_input, first_input + chunk - UNUSED


def tile_relativemultiheadattention_pa_t_kernel(tc, pos_embed, W_r_words, W_r_scales, b_r, out):
    nc = tc.nc
    x_dram = pos_embed.flatten_outer_dims()
    out_dram = out.flatten_outer_dims()

    with ExitStack() as ctx:
        const = ctx.enter_context(tc.tile_pool(name="const", bufs=1))
        x_pool = ctx.enter_context(tc.tile_pool(name="x", bufs=BATCH))
        result_pool = ctx.enter_context(tc.tile_pool(name="result", bufs=BATCH))
        grouped_pool = ctx.enter_context(tc.tile_pool(name="grouped", bufs=2))
        codes_pool = ctx.enter_context(tc.tile_pool(name="codes", bufs=3))
        flip_psum = ctx.enter_context(tc.psum_pool(name="flip", bufs=6))
        sum_psum = ctx.enter_context(tc.psum_pool(name="sum", bufs=2))
        ctx.enter_context(tc.manual_schedule())

        x_tiles = {}
        grouped_tiles = {}
        code_tiles = {}
        result_tiles = {}

        def load_slots(chunk, t, width):
            if t == 0:
                x_rows = x_pool.tile([P, SLOTS, D_IN], BF16, name="x_rows")
                x_tiles[chunk] = x_rows
            first_input = first_rows(chunk)[0]
            x_view = x_dram[first_input : first_input + SEQ, :].rearrange("(p t) k -> p t k", t=SLOTS)
            nc.sync.dma_start(
                out=x_tiles[chunk][:, t : t + width, :].rearrange("p t k -> p (t k)"),
                in_=x_view[:, t : t + width, :].rearrange("p t k -> p (t k)"),
            )

        def transpose_round(i):
            chunk, part = divmod(i, ROUNDS_PER_CHUNK)
            x_words = x_tiles[chunk][:].bitcast(F32)
            grouped = grouped_pool.tile([P, ROUND_SLOTS * D_IN], BF16, name="grouped", align_bytes=64)
            grouped_words = grouped[:].bitcast(F32).rearrange("p (t r u) -> p t r u", t=ROUND_SLOTS, u=2)
            for t in range(0, ROUND_SLOTS, SLOTS_PER_FLIP_BANK):
                flipped = flip_psum.tile([P, SLOTS_PER_FLIP_BANK, 2, P], F32, name="flipped")
                for s in range(SLOTS_PER_FLIP_BANK):
                    for u in range(2):
                        nc.tensor.transpose(
                            flipped[:, s, u, :], x_words[:, part * ROUND_SLOTS + t + s, u * P : (u + 1) * P], identity[:]
                        )
                nc.scalar.copy(
                    out=grouped_words[:, t : t + SLOTS_PER_FLIP_BANK, :, :],
                    in_=flipped[:].rearrange("p s u r -> p s r u"),
                )
            grouped_tiles[i] = grouped

        def quantise_round(i):
            grouped = grouped_tiles.pop(i)
            if i == ZERO_ROUND:
                by_row = grouped[:].rearrange("p (t r v) -> p t r v", t=ROUND_SLOTS, v=PACK)
                nc.vector.memset(by_row[:, ROUND_SLOTS - ZERO_ROWS :, P - 1, :], 0.0)
            codes = codes_pool.tile([P, ROUND_SLOTS * P], U32, name="codes", align_bytes=64)
            scales = codes_pool.tile([P, ROUND_SLOTS * P], U8, name="scales", align_bytes=64)
            width = SLOTS_PER_SUM_BANK * P
            for c in range(0, ROUND_SLOTS * P, width):
                nc.vector.quantize_mx(
                    out=codes[:, c : c + width].bitcast(FP8X4),
                    scales=scales[:, c : c + width],
                    in_=grouped[:, PACK * c : PACK * (c + width)],
                )
            code_tiles[i] = (codes, scales)

        def store(chunk, first_slot, slots, queue):
            first_output = first_rows(chunk)[1]
            out_view = out_dram[first_output : first_output + SEQ, :].rearrange("(p t) n -> p t n", t=SLOTS)
            queue.dma_start(
                out=out_view[:, first_slot : first_slot + slots, :],
                in_=result_tiles[chunk][:, first_slot : first_slot + slots, :],
            )

        def multiply_round(i):
            chunk, part = divmod(i, ROUNDS_PER_CHUNK)
            codes, scales = code_tiles.pop(i)
            if part == 0:
                result = result_pool.tile([P, SLOTS, D_OUT], F32, name="result")
                result_tiles[chunk] = result
            for t in range(0, ROUND_SLOTS, SLOTS_PER_SUM_BANK):
                sums = sum_psum.tile([P, SLOTS_PER_SUM_BANK, D_OUT], F32, name="sums")
                for s in range(SLOTS_PER_SUM_BANK):
                    cols = slice((t + s) * P, (t + s + 1) * P)
                    for h in range(2):
                        nc.tensor.matmul_mx(
                            out=sums[:, s, :],
                            lhsT=codes[:, cols].bitcast(FP8X4),
                            lhsT_scale=scales[:, cols],
                            rhs=w_half[:, 2 * D_OUT * h : 2 * D_OUT * (h + 1)].bitcast(FP4X4),
                            rhs_scale=w_scales[:, D_OUT * h : D_OUT * (h + 1)],
                            start=(h == 0),
                            stop=(h == 1),
                        )
                first_slot = part * ROUND_SLOTS + t
                nc.vector.tensor_tensor(
                    out=result_tiles[chunk][:, first_slot : first_slot + SLOTS_PER_SUM_BANK, :],
                    in0=sums[:],
                    in1=bias[:],
                    op=mybir.AluOpType.add,
                )
            if chunk == BATCH - 1:
                store(chunk, part * ROUND_SLOTS, ROUND_SLOTS, nc.sync)
            elif i == ZERO_ROUND:
                store(chunk, 0, SLOTS, nc.sync)
                second = 2 * (SEQ + 1) - DROPPED
                nc.sync.dma_start(
                    out=out_dram[second : second + (ZERO_ROWS - 2) * (SEQ + 1) + 1 : SEQ + 1, :].unsqueeze(0),
                    in_=result_tiles[chunk][P - 1 : P, FIRST_ZERO_SLOT + 1 :, :],
                )
            elif part == ROUNDS_PER_CHUNK - 1 and chunk != 1:
                store(chunk, 0, SLOTS, nc.sync)
                if chunk == 3:
                    store(1, 0, SLOTS, nc.sync)

        def spread_bias():
            spread = sum_psum.tile([P, SLOTS_PER_SUM_BANK, D_OUT], F32, name="sums")
            nc.tensor.matmul(
                out=spread[:].rearrange("p s n -> p (s n)"), lhsT=ones[:], rhs=bias_rows[:], start=True, stop=True
            )
            nc.vector.tensor_copy(out=bias[:], in_=spread[:])

        identity = const.tile([P, P], F32, name="identity")
        make_identity(nc, identity[:])
        w_raw = const.tile([P, D_OUT * 2], U8, name="w_raw", align_bytes=64)
        w_planes = const.tile([P, 2 * D_OUT], U8, name="w_planes", align_bytes=64)
        w_unzipped = const.tile([P, 2 * D_OUT], U8, name="w_unzipped", align_bytes=64)
        w_half = const.tile([P, 2 * D_OUT * 2], U8, name="w_half", align_bytes=64)
        w_scales = const.tile([P, 2 * D_OUT], U8, name="w_scales", align_bytes=64)
        ones = const.tile([P, P], BF16, name="ones")
        bias_rows = const.tile([P, SLOTS_PER_SUM_BANK * D_OUT], BF16, name="bias_rows")
        bias = const.tile([P, SLOTS_PER_SUM_BANK, D_OUT], F32, name="bias")
        nc.vector.memset(w_scales[:].bitcast(I32), 0)
        nc.vector.memset(w_half[:].bitcast(I32), 0)
        nc.vector.memset(ones[:], 1.0)
        nc.vector.memset(bias_rows[:], 0.0)

        nc.sync.dma_start(out=w_raw[:].bitcast(I32), in_=W_r_words[0].bitcast(I32))
        load_slots(0, 0, 2)
        scale_rows = W_r_scales[0].rearrange("(h g j) n -> j g h n", h=2, g=4, j=2)
        for i in range(4):
            nc.sync.dma_start(
                out=w_scales[i:P:32, :].bitcast(I32).rearrange("q (h m) -> q h m", h=2),
                in_=scale_rows[i // 2].bitcast(I32),
            )
        load_slots(0, 2, 6)
        load_slots(0, 8, 8)
        for c in range(2):
            nc.vector.tensor_copy(
                out=w_planes[:, D_OUT * c : D_OUT * (c + 1)], in_=w_raw[:].rearrange("p (n c) -> p n c", c=2)[:, :, c]
            )
        for h in range(2):
            for c in range(2):
                nc.sync.dma_start(
                    out=w_unzipped[c:P:2, D_OUT * h : D_OUT * (h + 1)].bitcast(I32),
                    in_=w_planes[64 * h : 64 * (h + 1), D_OUT * c : D_OUT * (c + 1)].bitcast(I32),
                )
        nc.gpsimd.dma_start(
            out=bias_rows[0:1, :].rearrange("o (s n) -> o s n", s=SLOTS_PER_SUM_BANK),
            in_=b_r.unsqueeze(0).unsqueeze(0).to_broadcast([1, SLOTS_PER_SUM_BANK, D_OUT]),
        )
        for chunk in (1, 2, 3):
            load_slots(chunk, 0, 8)
            load_slots(chunk, 8, 8)
        for chunk in range(4, BATCH):
            load_slots(chunk, 0, SLOTS)

        for step in range(ROUNDS + 2):
            if step < ROUNDS:
                transpose_round(step)
            if 1 <= step <= ROUNDS:
                quantise_round(step - 1)
            if step == 2:
                for h in range(2):
                    nc.vector.tensor_copy(
                        out=w_half[:, 2 * D_OUT * h : 2 * D_OUT * (h + 1)].rearrange("p (n c) -> p n c", c=2)[:, :, h],
                        in_=w_unzipped[:, D_OUT * h : D_OUT * (h + 1)],
                    )
                spread_bias()
            if step >= 2:
                multiply_round(step - 2)
